import numpy as np
import ml_dtypes


def mxq(x, axis, fmt="e4m3"):
    dtype, down = {"e4m3": (ml_dtypes.float8_e4m3fn, 7), "e5m2": (ml_dtypes.float8_e5m2, 14)}[fmt]
    v = np.moveaxis(np.asarray(x, np.float32).astype(ml_dtypes.bfloat16).astype(np.float64), axis, -1)
    blocks = v.reshape(v.shape[:-1] + (-1, 32))
    amax = np.abs(blocks).max(-1, keepdims=True)
    byte = np.maximum(np.where(amax > 0, np.frexp(amax)[1] - 1 + 127, 0) - down, 1)
    scale = np.exp2(byte - 127.0)
    codes = (blocks / scale).astype(np.float32).astype(dtype).astype(np.float64)
    return np.moveaxis((codes * scale).reshape(v.shape), -1, axis)


WIDE = False


def mx_kscale(k):
    if not WIDE:
        return np.ones(k)
    levels = np.array([10, -10, 5, -5, 0])
    a = np.random.permutation(np.resize(levels, k // 512 * 4)).reshape(k // 512, 4)
    idx = np.arange(k)
    return np.exp2(a[idx // 512, idx % 128 // 32])


BF16 = ml_dtypes.bfloat16


def bf(x):
    return np.asarray(x, np.float32).astype(BF16)


def f64(x):
    return np.asarray(x).astype(np.float64)


B, IN, H = 512, 1024, 1024


def sigmoid(v):
    return 1.0 / (1.0 + np.exp(-v))


def setup_inputs():
    s, t = mx_kscale(IN), mx_kscale(H)
    wsc = np.sqrt(2.0 / (IN + H))
    usc = 1.0 / np.sqrt(H)
    return {"joint_h": bf(np.random.standard_normal((B, H)) * t),
            "mgn_h": bf(np.random.standard_normal((B, IN)) * s),
            "W_r": bf(np.random.standard_normal((IN, H)) * wsc / s[:, None]),
            "W_h": bf(np.random.standard_normal((IN, H)) * wsc / s[:, None]),
            "U_r": bf(np.random.standard_normal((H, H)) * usc / t[:, None]),
            "U_h": bf(np.random.standard_normal((H, H)) * usc / t[:, None]),
            "b_r": bf(np.random.standard_normal(H) * 0.5),
            "b_h": bf(np.random.standard_normal(H) * 0.5)}


def reference(joint_h, mgn_h, W_r, W_h, U_r, U_h, b_r, b_h):
    h = f64(joint_h)
    xq = mxq(f64(mgn_h), 1, "e4m3")
    r = sigmoid((xq @ mxq(f64(W_r), 0, "e4m3")) + (mxq(h, 1, "e4m3") @ mxq(f64(U_r), 0, "e4m3")) + f64(b_r))
    g = h * r
    return np.tanh((xq @ mxq(f64(W_h), 0, "e4m3")) + (mxq(g, 1, "e4m3") @ mxq(f64(U_h), 0, "e4m3")) + f64(b_h))

@@ -1,0 +1,276 @@
+from contextlib import ExitStack
+
+import concourse.mybir as mybir
+from concourse.masks import make_identity
+
+FLOPS = 4 * 2 * 512 * 1024 * 1024
+
+F32 = mybir.dt.float32
+BF16 = mybir.dt.bfloat16
+I32 = mybir.dt.int32
+U32 = mybir.dt.uint32
+U8 = mybir.dt.uint8
+FP8X4 = mybir.dt.float8_e4m3fn_x4
+ACT = mybir.ActivationFunctionType
+ALU = mybir.AluOpType
+
+P = 128
+HALF = 512
+
+STEPS = (
+    ("Tx", "00"), ("Tx", "01"), ("Tx", "11"), ("Tx", "10"), ("Ex", "01", "S"), ("Th", "00"),
+    ("Ex", "00", "V"), ("Ex", "11", "V"), ("Qx", "1"), ("Eh", "00", "S"), ("Ex", "10", "V"), ("Th", "10"),
+    ("R", "Wr0a", "V"), ("Th", "01"), ("Eh", "10", "S"), ("Qx", "0"), ("Q", "Wr0a"), ("R", "Wr0b", "S"),
+    ("Q", "Wr0b"), ("Th", "11"), ("R", "Wr1b", "V"), ("Qh", "0"), ("R", "Ur0b", "V"), ("Eh", "01", "S"),
+    ("R", "Ur0a", "V"), ("Br", "0"), ("Bh", "0"), ("P1", "Wr0a"), ("Eh", "11", "S"), ("Q", "Ur0b"),
+    ("R", "Wr1a", "S"), ("R", "Ur1b", "S"), ("Q", "Ur0a"), ("R", "Ur1a", "V"), ("Q", "Wr1a"), ("P1", "Wr1a"),
+    ("P1", "Ur0a"), ("R", "Wh1a", "S"), ("Q", "Ur1b"), ("Qh", "1"), ("Q", "Wr1b"), ("R", "Wh0a", "S"),
+    ("Q", "Ur1a"), ("R", "Uh1a", "V"), ("P1", "Ur1a"), ("P1", "Ur0b"), ("Q", "Wh1a"), ("Sg", "1"),
+    ("Sg", "2"), ("Sg", "0"), ("Q", "Wh0a"), ("P1", "Wr1b"), ("Sg", "3"), ("P1", "Wr0b"),
+    ("R", "Wh1b", "V"), ("R", "Wh0b", "V"), ("P1", "Ur1b"), ("R", "Uh0a", "S"), ("Sg", "4"), ("G", "0"),
+    ("Sg", "5"), ("Q", "Wh1b"), ("Sg", "7"), ("Sg", "6"), ("Q", "Uh0a"), ("Q", "Wh0b"),
+    ("R", "Uh0b", "S"), ("R", "Uh1b", "S"), ("Qg", "0"), ("G", "1"), ("P2", "Wh1a"), ("P2", "Wh1b"),
+    ("P2", "Wh0a"), ("Q", "Uh1a"), ("P2", "Wh0b"), ("Qg", "1"), ("P2", "Uh0a"), ("Q", "Uh1b"),
+    ("P2", "Uh1a"), ("P2", "Uh1b"), ("Q", "Uh0b"), ("A", "01"), ("A", "03"), ("P2", "Uh0b"),
+    ("T", "01"), ("A", "02"), ("T", "03"), ("A", "11"), ("T", "02"), ("A", "12"),
+    ("A", "10"), ("T", "11"), ("A", "13"), ("T", "12"), ("A", "00"), ("T", "10"),
+    ("T", "13"), ("T", "00"),
+)
+
+WEIGHT = {"Wr": "W_r", "Ur": "U_r", "Wh": "W_h", "Uh": "U_h"}
+OPERAND = {"Wr": "x", "Ur": "h", "Wh": "x", "Uh": "g"}
+
+
+def tile_joint_gru_pa_kernel(tc, joint_h, mgn_h, W_r, W_h, U_r, U_h, b_r, b_h, out):
+    nc = tc.nc
+    dram = {"W_r": W_r, "W_h": W_h, "U_r": U_r, "U_h": U_h}
+    with ExitStack() as ctx:
+        const = ctx.enter_context(tc.tile_pool(name="const", bufs=1))
+        raw = ctx.enter_context(tc.tile_pool(name="raw", bufs=1))
+        keep = ctx.enter_context(tc.tile_pool(name="keep", bufs=1))
+        grp = ctx.enter_context(tc.tile_pool(name="grp", bufs=6))
+        outp = ctx.enter_context(tc.tile_pool(name="outp", bufs=8))
+        psum = ctx.enter_context(tc.psum_pool(name="psum", bufs=1))
+        ctx.enter_context(tc.manual_schedule())
+
+        def bank(i, shape, dtype, name):
+            return psum.tile(shape, dtype, name=name, tag="bank%d" % i)
+
+        br_rows = const.tile([P, P], BF16, name="br_rows")
+        nc.vector.memset(br_rows[:].bitcast(I32), 0)
+        bh_row = const.tile([P, 1024], BF16, name="bh_row")
+        nc.vector.memset(bh_row[:].bitcast(I32), 0)
+        warm = const.tile([P, 8], F32, name="warm")
+        nc.vector.memset(warm[:], 0.0)
+        nc.scalar.activation(out=warm[:, 4:5], in_=warm[:, 0:1], func=ACT.Sigmoid)
+        ident_f = const.tile([P, P], F32, name="ident_f")
+        make_identity(nc, ident_f[:])
+        ident_b = const.tile([P, P], BF16, name="ident_b")
+        make_identity(nc, ident_b[:])
+        ones_b = const.tile([P, P], BF16, name="ones_b")
+        nc.gpsimd.memset(ones_b[:], 1.0)
+
+        act_sb = {
+            "x": raw.tile([P, 4, 1024], BF16, name="x_sb"),
+            "h": raw.tile([P, 4, 1024], BF16, name="h_sb"),
+        }
+        wraw = {}
+        for name in ("W_r", "U_r", "W_h", "U_h"):
+            wraw[name] = raw.tile([P, 2, 4, 1024], BF16, name="raw_" + name)
+
+        for name, src in (("x", mgn_h), ("h", joint_h)):
+            rows = src.rearrange("(p a) k -> p a k", a=4)
+            for a2 in range(2):
+                nc.sync.dma_start(out=act_sb[name][:, 2 * a2 : 2 * a2 + 2, :], in_=rows[:, 2 * a2 : 2 * a2 + 2, :])
+        nc.sync.dma_start(out=br_rows[0:8, :], in_=b_r.rearrange("(m p) -> m p", p=P))
+        nc.sync.dma_start(out=bh_row[0:1, :], in_=b_h.rearrange("(o n) -> o n", o=1))
+        for g in range(2):
+            nc.sync.dma_start(
+                out=wraw["W_r"][:, g].rearrange("q (u e) n -> q u (e n)", u=2),
+                in_=W_r[512 * g : 512 * (g + 1), :].rearrange("(u q e) n -> q u (e n)", u=2, q=P, e=2),
+            )
+        for g in range(2):
+            nc.sync.dma_start(
+                out=wraw["U_r"][:, g], in_=U_r[512 * g : 512 * (g + 1), :].rearrange("(t p) n -> p t n", p=P)
+            )
+        for half in range(2):
+            cols = slice(HALF * half, HALF * (half + 1))
+            for e in range(2):
+                nc.sync.dma_start(
+                    out=wraw["W_h"][:].rearrange("q g (u e) n -> q (g u) e n", u=2)[:, :, e, cols],
+                    in_=W_h.rearrange("(c q e) n -> q c e n", c=4, q=P, e=2)[:, :, e, cols],
+                )
+            nc.sync.dma_start(
+                out=wraw["U_h"][:].rearrange("p g t n -> p (g t) n")[:, :, cols],
+                in_=U_h.rearrange("(c p) n -> p c n", p=P)[:, :, cols],
+            )
+
+        wc = {}
+        ws = {}
+        for name in ("W_r", "U_r", "W_h", "U_h"):
+            wc[name] = keep.tile([P, 2, 1024], U32, name="codes_" + name, align_bytes=64)
+            ws[name] = keep.tile([P, 2, 1024], U8, name="scales_" + name, align_bytes=64)
+        ac = {}
+        asc = {}
+        ag = {}
+        for name in ("x", "h", "g"):
+            ac[name] = keep.tile([P, 2, HALF], U32, name="codes_" + name, align_bytes=64)
+            asc[name] = keep.tile([P, 2, HALF], U8, name="scales_" + name, align_bytes=64)
+            ag[name] = [
+                keep.tile([P, 4 * HALF], BF16, name="grouped_%s%d" % (name, g), align_bytes=64)
+                for g in range(2)
+            ]
+        r_sb = keep.tile([P, 8, HALF], F32, name="r_sb")
+        br_col = const.tile([P, 8], F32, name="br_col")
+        bh_bc = const.tile([P, 1024], BF16, name="bh_bc")
+        out_rows = out.rearrange("(p a) n -> p a n", a=4)
+
+        first = {}
+        last = {}
+        for i, step in enumerate(STEPS):
+            if step[0] == "P1" or step[0] == "P2":
+                key = (step[0], step[1][3])
+                if key not in first:
+                    first[key] = i
+                last[key] = i
+
+        def copy(engine, dst, src):
+            if engine == "V":
+                nc.vector.tensor_copy(out=dst, in_=src)
+            else:
+                nc.scalar.copy(out=dst, in_=src)
+
+        grouped_of = {}
+        banks = {}
+        z_of = {}
+        for i, step in enumerate(STEPS):
+            op = step[0]
+            arg = step[1]
+            if op == "R":
+                name, g, half = WEIGHT[arg[0:2]], int(arg[2]), "ab".index(arg[3])
+                grouped = grp.tile([P, HALF, 4], BF16, name="grouped", tag="grouped", align_bytes=64)
+                grouped_of[arg] = grouped
+                copy(
+                    step[2],
+                    grouped[:].rearrange("p (c i) t -> p c t i", i=4),
+                    wraw[name][:, g, :, HALF * half : HALF * (half + 1)].rearrange("p t (c i) -> p c t i", i=4),
+                )
+            elif op == "Q":
+                name, g, half = WEIGHT[arg[0:2]], int(arg[2]), "ab".index(arg[3])
+                cols = slice(HALF * half, HALF * (half + 1))
+                nc.vector.quantize_mx(
+                    out=wc[name][:, g, cols].bitcast(FP8X4),
+                    scales=ws[name][:, g, cols],
+                    in_=grouped_of[arg][:].rearrange("p w t -> p (w t)"),
+                )
+            elif op == "Tx":
+                a2, g = int(arg[0]), int(arg[1])
+                xt = bank(2 * a2 + g, [P, 2, 2, P], F32, "xt")
+                banks[("x", arg)] = xt
+                for c in range(2):
+                    words = act_sb["x"][:, 2 * a2 + c, :].bitcast(F32)
+                    for u in range(2):
+                        w0 = P * (2 * g + u)
+                        nc.tensor.transpose(xt[:, c, u, :], words[:, w0 : w0 + P], ident_f[:])
+            elif op == "Ex":
+                a2, g = int(arg[0]), int(arg[1])
+                copy(
+                    step[2],
+                    ag["x"][g][:]
+                    .bitcast(F32)[:, 512 * a2 : 512 * (a2 + 1)]
+                    .rearrange("q (c b u) -> q c b u", c=2, b=P, u=2),
+                    banks[("x", arg)][:].rearrange("q c u b -> q c b u"),
+                )
+            elif op == "Th":
+                a2, g = int(arg[0]), int(arg[1])
+                ht = bank(4 + 2 * a2 + g, [P, 2, 4, P], BF16, "ht")
+                banks[("h", arg)] = ht
+                for c in range(2):
+                    for t in range(4):
+                        k0 = 512 * g + P * t
+                        nc.tensor.transpose(ht[:, c, t, :], act_sb["h"][:, 2 * a2 + c, k0 : k0 + P], ident_b[:])
+            elif op == "Eh":
+                a2, g = int(arg[0]), int(arg[1])
+                copy(
+                    step[2],
+                    ag["h"][g][:, 1024 * a2 : 1024 * (a2 + 1)].rearrange("p (c b t) -> p c b t", c=2, b=P, t=4),
+                    banks[("h", arg)][:].rearrange("p c t b -> p c b t"),
+                )
+            elif op == "Qx" or op == "Qh" or op == "Qg":
+                name, g = op[1], int(arg)
+                nc.vector.quantize_mx(
+                    out=ac[name][:, g, :].bitcast(FP8X4), scales=asc[name][:, g, :], in_=ag[name][g][:]
+                )
+            elif op == "Br":
+                br_ps = bank(0, [P, P], BF16, "br_ps")
+                nc.tensor.transpose(br_ps[:], br_rows[:], ident_b[:])
+                nc.vector.tensor_copy(out=br_col[:], in_=br_ps[:, 0:8])
+            elif op == "Bh":
+                bh_ps = bank(1, [P, 1024], BF16, "bh_ps")
+                for j in range(2):
+                    nc.tensor.matmul(
+                        out=bh_ps[:, HALF * j : HALF * (j + 1)],
+                        lhsT=ones_b[:],
+                        rhs=bh_row[:, HALF * j : HALF * (j + 1)],
+                        start=True,
+                        stop=True,
+                    )
+                nc.scalar.copy(out=bh_bc[:], in_=bh_ps[:])
+            elif op == "P1":
+                name, an, g, half = WEIGHT[arg[0:2]], OPERAND[arg[0:2]], int(arg[2]), "ab".index(arg[3])
+                for m in range(4 * half, 4 * half + 4):
+                    if first[(op, arg[3])] == i:
+                        banks[("acc1", m)] = bank(m, [P, HALF], F32, "acc1")
+                    nc.tensor.matmul_mx(
+                        out=banks[("acc1", m)][:],
+                        lhsT=wc[name][:, g, P * m : P * (m + 1)].bitcast(FP8X4),
+                        lhsT_scale=ws[name][:, g, P * m : P * (m + 1)],
+                        rhs=ac[an][:, g, :].bitcast(FP8X4),
+                        rhs_scale=asc[an][:, g, :],
+                        start=(first[(op, arg[3])] == i),
+                        stop=(last[(op, arg[3])] == i),
+                    )
+            elif op == "Sg":
+                m = int(arg)
+                nc.scalar.activation(
+                    out=r_sb[:, m, :],
+                    in_=banks[("acc1", m)][:],
+                    func=ACT.Sigmoid,
+                    bias=br_col[:, m : m + 1],
+                    scale=1.0,
+                )
+            elif op == "G":
+                g2 = int(arg)
+                nc.vector.tensor_tensor(
+                    out=ag["g"][g2][:].rearrange("p (b t) -> p b t", t=4),
+                    in0=r_sb[:, 4 * g2 : 4 * g2 + 4, :].rearrange("p t b -> p b t"),
+                    in1=ag["h"][g2][:].rearrange("p (b t) -> p b t", t=4),
+                    op=ALU.mult,
+                )
+            elif op == "P2":
+                name, an, g, j = WEIGHT[arg[0:2]], OPERAND[arg[0:2]], int(arg[2]), "ab".index(arg[3])
+                cols = slice(HALF * j, HALF * (j + 1))
+                for a in range(4):
+                    if first[(op, arg[3])] == i:
+                        banks[("acc2", j, a)] = bank(4 * j + a, [P, HALF], F32, "acc2")
+                    nc.tensor.matmul_mx(
+                        out=banks[("acc2", j, a)][:],
+                        lhsT=ac[an][:, g, P * a : P * (a + 1)].bitcast(FP8X4),
+                        lhsT_scale=asc[an][:, g, P * a : P * (a + 1)],
+                        rhs=wc[name][:, g, cols].bitcast(FP8X4),
+                        rhs_scale=ws[name][:, g, cols],
+                        start=(first[(op, arg[3])] == i),
+                        stop=(last[(op, arg[3])] == i),
+                    )
+            elif op == "A":
+                j, a = int(arg[0]), int(arg[1])
+                z = outp.tile([P, HALF], F32, name="z", tag="z")
+                z_of[arg] = z
+                nc.vector.tensor_tensor(
+                    out=z[:], in0=banks[("acc2", j, a)][:], in1=bh_bc[:, HALF * j : HALF * (j + 1)], op=ALU.add
+                )
+            elif op == "T":
+                j, a = int(arg[0]), int(arg[1])
+                z = z_of[arg]
+                nc.scalar.activation(out=z[:], in_=z[:], func=ACT.Tanh)
+                nc.sync.dma_start(out=out_rows[:, a, HALF * j : HALF * (j + 1)], in_=z[:])

@@ -120,7 +120,7 @@ def tile_joint_gru_pa_kernel(tc, joint_h, mgn_h, W_r, W_h, U_r, U_h, b_r, b_h, o
                 keep.tile([P, 4 * HALF], BF16, name="grouped_%s%d" % (name, g), align_bytes=64)
                 for g in range(2)
             ]
-        r_sb = keep.tile([P, 8, HALF], F32, name="r_sb")
+        r_sb = [keep.tile([P, P, 4, 4], F32, name="r_sb%d" % g) for g in range(2)]
         br_col = const.tile([P, 8], F32, name="br_col")
         bh_bc = const.tile([P, 1024], BF16, name="bh_bc")
         out_rows = out.rearrange("(p a) n -> p a n", a=4)
@@ -233,8 +233,8 @@ def tile_joint_gru_pa_kernel(tc, joint_h, mgn_h, W_r, W_h, U_r, U_h, b_r, b_h, o
             elif op == "Sg":
                 m = int(arg)
                 nc.scalar.activation(
-                    out=r_sb[:, m, :],
-                    in_=banks[("acc1", m)][:],
+                    out=r_sb[m // 4][:, :, m % 4, :],
+                    in_=banks[("acc1", m)][:].rearrange("p (c i) -> p c i", i=4),
                     func=ACT.Sigmoid,
                     bias=br_col[:, m : m + 1],
                     scale=1.0,
@@ -242,9 +242,9 @@ def tile_joint_gru_pa_kernel(tc, joint_h, mgn_h, W_r, W_h, U_r, U_h, b_r, b_h, o
             elif op == "G":
                 g2 = int(arg)
                 nc.vector.tensor_tensor(
-                    out=ag["g"][g2][:].rearrange("p (b t) -> p b t", t=4),
-                    in0=r_sb[:, 4 * g2 : 4 * g2 + 4, :].rearrange("p t b -> p b t"),
-                    in1=ag["h"][g2][:].rearrange("p (b t) -> p b t", t=4),
+                    out=ag["g"][g2][:].rearrange("p (c i t) -> p c t i", i=4, t=4),
+                    in0=r_sb[g2][:],
+                    in1=ag["h"][g2][:].rearrange("p (c i t) -> p c t i", i=4, t=4),
                     op=ALU.mult,
                 )
             elif op == "P2":

@@ -15,41 +15,36 @@ ACT = mybir.ActivationFunctionType
 ALU = mybir.AluOpType
 
 P = 128
-HALF = 512
+PACK = 4
+PASSES = 2
+BATCH = 512
+WIDTH = 1024
+UNIT = 512
+TILES = UNIT // P
 
-STEPS = (
-    ("Tx", "00"), ("Tx", "01"), ("Tx", "11"), ("Tx", "10"), ("Ex", "01", "S"), ("Th", "00"),
-    ("Ex", "00", "V"), ("Ex", "11", "V"), ("Qx", "1"), ("Eh", "00", "S"), ("Ex", "10", "V"), ("Th", "10"),
-    ("R", "Wr0a", "V"), ("Th", "01"), ("Eh", "10", "S"), ("Qx", "0"), ("Q", "Wr0a"), ("R", "Wr0b", "S"),
-    ("Q", "Wr0b"), ("Th", "11"), ("R", "Wr1b", "V"), ("Qh", "0"), ("R", "Ur0b", "V"), ("Eh", "01", "S"),
-    ("R", "Ur0a", "V"), ("Br", "0"), ("Bh", "0"), ("P1", "Wr0a"), ("Eh", "11", "S"), ("Q", "Ur0b"),
-    ("R", "Wr1a", "S"), ("R", "Ur1b", "S"), ("Q", "Ur0a"), ("R", "Ur1a", "V"), ("Q", "Wr1a"), ("P1", "Wr1a"),
-    ("P1", "Ur0a"), ("R", "Wh1a", "S"), ("Q", "Ur1b"), ("Qh", "1"), ("Q", "Wr1b"), ("R", "Wh0a", "S"),
-    ("Q", "Ur1a"), ("R", "Uh1a", "V"), ("P1", "Ur1a"), ("P1", "Ur0b"), ("Q", "Wh1a"), ("Sg", "1"),
-    ("Sg", "2"), ("Sg", "0"), ("Q", "Wh0a"), ("P1", "Wr1b"), ("Sg", "3"), ("P1", "Wr0b"),
-    ("R", "Wh1b", "V"), ("R", "Wh0b", "V"), ("P1", "Ur1b"), ("R", "Uh0a", "S"), ("Sg", "4"), ("G", "0"),
-    ("Sg", "5"), ("Q", "Wh1b"), ("Sg", "7"), ("Sg", "6"), ("Q", "Uh0a"), ("Q", "Wh0b"),
-    ("R", "Uh0b", "S"), ("R", "Uh1b", "S"), ("Qg", "0"), ("G", "1"), ("P2", "Wh1a"), ("P2", "Wh1b"),
-    ("P2", "Wh0a"), ("Q", "Uh1a"), ("P2", "Wh0b"), ("Qg", "1"), ("P2", "Uh0a"), ("Q", "Uh1b"),
-    ("P2", "Uh1a"), ("P2", "Uh1b"), ("Q", "Uh0b"), ("A", "01"), ("A", "03"), ("P2", "Uh0b"),
-    ("T", "01"), ("A", "02"), ("T", "03"), ("A", "11"), ("T", "02"), ("A", "12"),
-    ("A", "10"), ("T", "11"), ("A", "13"), ("T", "12"), ("A", "00"), ("T", "10"),
-    ("T", "13"), ("T", "00"),
-)
+UNITS = [(name, g, half) for name in ("W_r", "U_r", "W_h", "U_h") for g in range(PASSES) for half in range(2)]
+MOVING_WITH = {"W_r": "x", "U_r": "h", "W_h": "x", "U_h": "g"}
+STAGE_2 = 8
 
-WEIGHT = {"Wr": "W_r", "Ur": "U_r", "Wh": "W_h", "Uh": "U_h"}
-OPERAND = {"Wr": "x", "Ur": "h", "Wh": "x", "Uh": "g"}
+VECTOR_SHARE = 224
+
+
+def vector_share(i):
+    if i in (STAGE_2, STAGE_2 + 1):
+        return UNIT
+    if i in (STAGE_2 + 2, STAGE_2 + 3):
+        return 0
+    return VECTOR_SHARE
 
 
 def tile_joint_gru_pa_kernel(tc, joint_h, mgn_h, W_r, W_h, U_r, U_h, b_r, b_h, out):
     nc = tc.nc
-    dram = {"W_r": W_r, "W_h": W_h, "U_r": U_r, "U_h": U_h}
     with ExitStack() as ctx:
         const = ctx.enter_context(tc.tile_pool(name="const", bufs=1))
         raw = ctx.enter_context(tc.tile_pool(name="raw", bufs=1))
         keep = ctx.enter_context(tc.tile_pool(name="keep", bufs=1))
-        grp = ctx.enter_context(tc.tile_pool(name="grp", bufs=6))
-        outp = ctx.enter_context(tc.tile_pool(name="outp", bufs=8))
+        regrouped = ctx.enter_context(tc.tile_pool(name="regrouped", bufs=6))
+        results = ctx.enter_context(tc.tile_pool(name="results", bufs=8))
         psum = ctx.enter_context(tc.psum_pool(name="psum", bufs=1))
         ctx.enter_context(tc.manual_schedule())
 
@@ -58,7 +53,7 @@ def tile_joint_gru_pa_kernel(tc, joint_h, mgn_h, W_r, W_h, U_r, U_h, b_r, b_h, o
 
         br_rows = const.tile([P, P], BF16, name="br_rows")
         nc.vector.memset(br_rows[:].bitcast(I32), 0)
-        bh_row = const.tile([P, 1024], BF16, name="bh_row")
+        bh_row = const.tile([P, WIDTH], BF16, name="bh_row")
         nc.vector.memset(bh_row[:].bitcast(I32), 0)
         warm = const.tile([P, 8], F32, name="warm")
         nc.vector.memset(warm[:], 0.0)
@@ -70,207 +65,210 @@ def tile_joint_gru_pa_kernel(tc, joint_h, mgn_h, W_r, W_h, U_r, U_h, b_r, b_h, o
         ones_b = const.tile([P, P], BF16, name="ones_b")
         nc.gpsimd.memset(ones_b[:], 1.0)
 
-        act_sb = {
-            "x": raw.tile([P, 4, 1024], BF16, name="x_sb"),
-            "h": raw.tile([P, 4, 1024], BF16, name="h_sb"),
-        }
-        wraw = {}
-        for name in ("W_r", "U_r", "W_h", "U_h"):
-            wraw[name] = raw.tile([P, 2, 4, 1024], BF16, name="raw_" + name)
-
+        act_raw = {}
         for name, src in (("x", mgn_h), ("h", joint_h)):
-            rows = src.rearrange("(p a) k -> p a k", a=4)
-            for a2 in range(2):
-                nc.sync.dma_start(out=act_sb[name][:, 2 * a2 : 2 * a2 + 2, :], in_=rows[:, 2 * a2 : 2 * a2 + 2, :])
-        nc.sync.dma_start(out=br_rows[0:8, :], in_=b_r.rearrange("(m p) -> m p", p=P))
+            act_raw[name] = raw.tile([P, TILES, WIDTH], BF16, name="raw_" + name)
+            rows = src.rearrange("(p a) k -> p a k", a=TILES)
+            for pair in range(2):
+                nc.sync.dma_start(out=act_raw[name][:, 2 * pair : 2 * pair + 2, :], in_=rows[:, 2 * pair : 2 * pair + 2, :])
+        nc.sync.dma_start(out=br_rows[0 : WIDTH // P, :], in_=b_r.rearrange("(m p) -> m p", p=P))
         nc.sync.dma_start(out=bh_row[0:1, :], in_=b_h.rearrange("(o n) -> o n", o=1))
-        for g in range(2):
-            nc.sync.dma_start(
-                out=wraw["W_r"][:, g].rearrange("q (u e) n -> q u (e n)", u=2),
-                in_=W_r[512 * g : 512 * (g + 1), :].rearrange("(u q e) n -> q u (e n)", u=2, q=P, e=2),
-            )
-        for g in range(2):
-            nc.sync.dma_start(
-                out=wraw["U_r"][:, g], in_=U_r[512 * g : 512 * (g + 1), :].rearrange("(t p) n -> p t n", p=P)
-            )
-        for half in range(2):
-            cols = slice(HALF * half, HALF * (half + 1))
-            for e in range(2):
-                nc.sync.dma_start(
-                    out=wraw["W_h"][:].rearrange("q g (u e) n -> q (g u) e n", u=2)[:, :, e, cols],
-                    in_=W_h.rearrange("(c q e) n -> q c e n", c=4, q=P, e=2)[:, :, e, cols],
-                )
-            nc.sync.dma_start(
-                out=wraw["U_h"][:].rearrange("p g t n -> p (g t) n")[:, :, cols],
-                in_=U_h.rearrange("(c p) n -> p c n", p=P)[:, :, cols],
-            )
+        weight_raw = {}
+        for name, src in (("W_r", W_r), ("U_r", U_r), ("W_h", W_h), ("U_h", U_h)):
+            weight_raw[name] = raw.tile([P, PASSES, PACK, WIDTH], BF16, name="raw_" + name)
+            for g in range(PASSES):
+                rows = src[UNIT * g : UNIT * (g + 1), :]
+                if name[0] == "W":
+                    nc.sync.dma_start(
+                        out=weight_raw[name][:, g].rearrange("q (u e) n -> q u (e n)", u=2),
+                        in_=rows.rearrange("(u q e) n -> q u (e n)", u=2, q=P, e=2),
+                    )
+                else:
+                    nc.sync.dma_start(out=weight_raw[name][:, g], in_=rows.rearrange("(t p) n -> p t n", p=P))
 
-        wc = {}
-        ws = {}
+        words = {}
+        scales = {}
         for name in ("W_r", "U_r", "W_h", "U_h"):
-            wc[name] = keep.tile([P, 2, 1024], U32, name="codes_" + name, align_bytes=64)
-            ws[name] = keep.tile([P, 2, 1024], U8, name="scales_" + name, align_bytes=64)
-        ac = {}
-        asc = {}
-        ag = {}
+            words[name] = keep.tile([P, PASSES, WIDTH], U32, name="words_" + name, align_bytes=64)
+            scales[name] = keep.tile([P, PASSES, WIDTH], U8, name="scales_" + name, align_bytes=64)
+        grouped = {}
         for name in ("x", "h", "g"):
-            ac[name] = keep.tile([P, 2, HALF], U32, name="codes_" + name, align_bytes=64)
-            asc[name] = keep.tile([P, 2, HALF], U8, name="scales_" + name, align_bytes=64)
-            ag[name] = [
-                keep.tile([P, 4 * HALF], BF16, name="grouped_%s%d" % (name, g), align_bytes=64)
-                for g in range(2)
+            words[name] = keep.tile([P, PASSES, BATCH], U32, name="words_" + name, align_bytes=64)
+            scales[name] = keep.tile([P, PASSES, BATCH], U8, name="scales_" + name, align_bytes=64)
+            grouped[name] = [
+                keep.tile([P, PACK * BATCH], BF16, name="grouped_%s%d" % (name, g), align_bytes=64)
+                for g in range(PASSES)
             ]
-        r_sb = [keep.tile([P, P, 4, 4], F32, name="r_sb%d" % g) for g in range(2)]
-        br_col = const.tile([P, 8], F32, name="br_col")
-        bh_bc = const.tile([P, 1024], BF16, name="bh_bc")
-        out_rows = out.rearrange("(p a) n -> p a n", a=4)
 
-        first = {}
-        last = {}
-        for i, step in enumerate(STEPS):
-            if step[0] == "P1" or step[0] == "P2":
-                key = (step[0], step[1][3])
-                if key not in first:
-                    first[key] = i
-                last[key] = i
+        def quantise_activation(name, g):
+            nc.vector.quantize_mx(
+                out=words[name][:, g, :].bitcast(FP8X4), scales=scales[name][:, g, :], in_=grouped[name][g][:]
+            )
 
         def copy(engine, dst, src):
-            if engine == "V":
+            if engine == "vector":
                 nc.vector.tensor_copy(out=dst, in_=src)
             else:
                 nc.scalar.copy(out=dst, in_=src)
 
-        grouped_of = {}
-        banks = {}
-        z_of = {}
-        for i, step in enumerate(STEPS):
-            op = step[0]
-            arg = step[1]
-            if op == "R":
-                name, g, half = WEIGHT[arg[0:2]], int(arg[2]), "ab".index(arg[3])
-                grouped = grp.tile([P, HALF, 4], BF16, name="grouped", tag="grouped", align_bytes=64)
-                grouped_of[arg] = grouped
-                copy(
-                    step[2],
-                    grouped[:].rearrange("p (c i) t -> p c t i", i=4),
-                    wraw[name][:, g, :, HALF * half : HALF * (half + 1)].rearrange("p t (c i) -> p c t i", i=4),
-                )
-            elif op == "Q":
-                name, g, half = WEIGHT[arg[0:2]], int(arg[2]), "ab".index(arg[3])
-                cols = slice(HALF * half, HALF * (half + 1))
-                nc.vector.quantize_mx(
-                    out=wc[name][:, g, cols].bitcast(FP8X4),
-                    scales=ws[name][:, g, cols],
-                    in_=grouped_of[arg][:].rearrange("p w t -> p (w t)"),
-                )
-            elif op == "Tx":
-                a2, g = int(arg[0]), int(arg[1])
-                xt = bank(2 * a2 + g, [P, 2, 2, P], F32, "xt")
-                banks[("x", arg)] = xt
+        transposed = {}
+        for pair in range(2):
+            for g in range(PASSES):
+                xt = bank(2 * pair + g, [P, 2, 2, P], F32, "xt")
+                transposed[("x", pair, g)] = xt
                 for c in range(2):
-                    words = act_sb["x"][:, 2 * a2 + c, :].bitcast(F32)
+                    pairs_of_k = act_raw["x"][:, 2 * pair + c, :].bitcast(F32)
                     for u in range(2):
-                        w0 = P * (2 * g + u)
-                        nc.tensor.transpose(xt[:, c, u, :], words[:, w0 : w0 + P], ident_f[:])
-            elif op == "Ex":
-                a2, g = int(arg[0]), int(arg[1])
-                copy(
-                    step[2],
-                    ag["x"][g][:]
-                    .bitcast(F32)[:, 512 * a2 : 512 * (a2 + 1)]
-                    .rearrange("q (c b u) -> q c b u", c=2, b=P, u=2),
-                    banks[("x", arg)][:].rearrange("q c u b -> q c b u"),
-                )
-            elif op == "Th":
-                a2, g = int(arg[0]), int(arg[1])
-                ht = bank(4 + 2 * a2 + g, [P, 2, 4, P], BF16, "ht")
-                banks[("h", arg)] = ht
+                        first = P * (2 * g + u)
+                        nc.tensor.transpose(xt[:, c, u, :], pairs_of_k[:, first : first + P], ident_f[:])
+        for pair in range(2):
+            for g in range(PASSES):
+                ht = bank(4 + 2 * pair + g, [P, 2, PACK, P], BF16, "ht")
+                transposed[("h", pair, g)] = ht
                 for c in range(2):
-                    for t in range(4):
-                        k0 = 512 * g + P * t
-                        nc.tensor.transpose(ht[:, c, t, :], act_sb["h"][:, 2 * a2 + c, k0 : k0 + P], ident_b[:])
-            elif op == "Eh":
-                a2, g = int(arg[0]), int(arg[1])
-                copy(
-                    step[2],
-                    ag["h"][g][:, 1024 * a2 : 1024 * (a2 + 1)].rearrange("p (c b t) -> p c b t", c=2, b=P, t=4),
-                    banks[("h", arg)][:].rearrange("p c t b -> p c b t"),
-                )
-            elif op == "Qx" or op == "Qh" or op == "Qg":
-                name, g = op[1], int(arg)
-                nc.vector.quantize_mx(
-                    out=ac[name][:, g, :].bitcast(FP8X4), scales=asc[name][:, g, :], in_=ag[name][g][:]
-                )
-            elif op == "Br":
-                br_ps = bank(0, [P, P], BF16, "br_ps")
-                nc.tensor.transpose(br_ps[:], br_rows[:], ident_b[:])
-                nc.vector.tensor_copy(out=br_col[:], in_=br_ps[:, 0:8])
-            elif op == "Bh":
-                bh_ps = bank(1, [P, 1024], BF16, "bh_ps")
-                for j in range(2):
-                    nc.tensor.matmul(
-                        out=bh_ps[:, HALF * j : HALF * (j + 1)],
-                        lhsT=ones_b[:],
-                        rhs=bh_row[:, HALF * j : HALF * (j + 1)],
-                        start=True,
-                        stop=True,
+                    for t in range(PACK):
+                        first = UNIT * g + P * t
+                        nc.tensor.transpose(ht[:, c, t, :], act_raw["h"][:, 2 * pair + c, first : first + P], ident_b[:])
+
+        def evacuate(name, pair):
+            for g, engine in enumerate(("vector", "scalar")):
+                if name == "x":
+                    copy(
+                        engine,
+                        grouped["x"][g][:]
+                        .bitcast(F32)[:, UNIT * pair : UNIT * (pair + 1)]
+                        .rearrange("q (c b u) -> q c b u", c=2, b=P, u=2),
+                        transposed[("x", pair, g)][:].rearrange("q c u b -> q c b u"),
                     )
-                nc.scalar.copy(out=bh_bc[:], in_=bh_ps[:])
-            elif op == "P1":
-                name, an, g, half = WEIGHT[arg[0:2]], OPERAND[arg[0:2]], int(arg[2]), "ab".index(arg[3])
-                for m in range(4 * half, 4 * half + 4):
-                    if first[(op, arg[3])] == i:
-                        banks[("acc1", m)] = bank(m, [P, HALF], F32, "acc1")
-                    nc.tensor.matmul_mx(
-                        out=banks[("acc1", m)][:],
-                        lhsT=wc[name][:, g, P * m : P * (m + 1)].bitcast(FP8X4),
-                        lhsT_scale=ws[name][:, g, P * m : P * (m + 1)],
-                        rhs=ac[an][:, g, :].bitcast(FP8X4),
-                        rhs_scale=asc[an][:, g, :],
-                        start=(first[(op, arg[3])] == i),
-                        stop=(last[(op, arg[3])] == i),
+                else:
+                    copy(
+                        engine,
+                        grouped["h"][g][:, 2 * UNIT * pair : 2 * UNIT * (pair + 1)].rearrange(
+                            "p (c b t) -> p c b t", c=2, b=P, t=PACK
+                        ),
+                        transposed[("h", pair, g)][:].rearrange("p c t b -> p c b t"),
                     )
-            elif op == "Sg":
-                m = int(arg)
+
+        evacuate("x", 0)
+        evacuate("x", 1)
+        quantise_activation("x", 0)
+        quantise_activation("x", 1)
+
+        br_ps = bank(0, [P, P], BF16, "br_ps")
+        nc.tensor.transpose(br_ps[:], br_rows[:], ident_b[:])
+        br_col = const.tile([P, WIDTH // P], F32, name="br_col")
+        nc.vector.tensor_copy(out=br_col[:], in_=br_ps[:, 0 : WIDTH // P])
+        bh_ps = bank(1, [P, WIDTH], BF16, "bh_ps")
+        for j in range(2):
+            nc.tensor.matmul(
+                out=bh_ps[:, UNIT * j : UNIT * (j + 1)],
+                lhsT=ones_b[:],
+                rhs=bh_row[:, UNIT * j : UNIT * (j + 1)],
+                start=True,
+                stop=True,
+            )
+        bh_all = const.tile([P, WIDTH], BF16, name="bh_all")
+        nc.scalar.copy(out=bh_all[:], in_=bh_ps[:])
+
+        unit_tile = {}
+
+        def regroup(i):
+            name, g, half = UNITS[i]
+            unit_tile[i] = regrouped.tile([P, UNIT, PACK], BF16, name="unit", tag="unit", align_bytes=64)
+            split = vector_share(i)
+            for engine, lo, hi in (("scalar", split, UNIT), ("vector", 0, split)):
+                if lo < hi:
+                    copy(
+                        engine,
+                        unit_tile[i][:, lo:hi, :].rearrange("p (c i) t -> p c t i", i=4),
+                        weight_raw[name][:, g, :, UNIT * half + lo : UNIT * half + hi].rearrange(
+                            "p t (c i) -> p c t i", i=4
+                        ),
+                    )
+
+        def quantise(i):
+            name, g, half = UNITS[i]
+            cols = slice(UNIT * half, UNIT * (half + 1))
+            nc.vector.quantize_mx(
+                out=words[name][:, g, cols].bitcast(FP8X4),
+                scales=scales[name][:, g, cols],
+                in_=unit_tile[i][:].rearrange("p n t -> p (n t)"),
+            )
+
+        sums = {}
+
+        def multiply(i):
+            name, g, half = UNITS[i]
+            act = MOVING_WITH[name]
+            opens = name[0] == "W" and g == 0
+            closes = name[0] == "U" and g == PASSES - 1
+            for tile in range(TILES):
+                if i < STAGE_2:
+                    key = ("r", TILES * half + tile)
+                    stationary, s_cols = name, slice(UNIT * half + P * tile, UNIT * half + P * (tile + 1))
+                    moving, m_cols = act, slice(0, BATCH)
+                else:
+                    key = ("out", half, tile)
+                    stationary, s_cols = act, slice(P * tile, P * (tile + 1))
+                    moving, m_cols = name, slice(UNIT * half, UNIT * (half + 1))
+                if opens:
+                    sums[key] = bank(TILES * half + tile, [P, UNIT], F32, "sums")
+                nc.tensor.matmul_mx(
+                    out=sums[key][:],
+                    lhsT=words[stationary][:, g, s_cols].bitcast(FP8X4),
+                    lhsT_scale=scales[stationary][:, g, s_cols],
+                    rhs=words[moving][:, g, m_cols].bitcast(FP8X4),
+                    rhs_scale=scales[moving][:, g, m_cols],
+                    start=opens,
+                    stop=closes,
+                )
+
+        r_runs = [keep.tile([P, BATCH // 4, PACK, 4], F32, name="r_runs%d" % g) for g in range(PASSES)]
+
+        def sigmoid(half):
+            for t in range(TILES):
+                m = TILES * half + t
                 nc.scalar.activation(
-                    out=r_sb[m // 4][:, :, m % 4, :],
-                    in_=banks[("acc1", m)][:].rearrange("p (c i) -> p c i", i=4),
+                    out=r_runs[half][:, :, t, :],
+                    in_=sums[("r", m)][:].rearrange("p (c i) -> p c i", i=4),
                     func=ACT.Sigmoid,
                     bias=br_col[:, m : m + 1],
                     scale=1.0,
                 )
-            elif op == "G":
-                g2 = int(arg)
-                nc.vector.tensor_tensor(
-                    out=ag["g"][g2][:].rearrange("p (c i t) -> p c t i", i=4, t=4),
-                    in0=r_sb[g2][:],
-                    in1=ag["h"][g2][:].rearrange("p (c i t) -> p c t i", i=4, t=4),
-                    op=ALU.mult,
-                )
-            elif op == "P2":
-                name, an, g, j = WEIGHT[arg[0:2]], OPERAND[arg[0:2]], int(arg[2]), "ab".index(arg[3])
-                cols = slice(HALF * j, HALF * (j + 1))
-                for a in range(4):
-                    if first[(op, arg[3])] == i:
-                        banks[("acc2", j, a)] = bank(4 * j + a, [P, HALF], F32, "acc2")
-                    nc.tensor.matmul_mx(
-                        out=banks[("acc2", j, a)][:],
-                        lhsT=ac[an][:, g, P * a : P * (a + 1)].bitcast(FP8X4),
-                        lhsT_scale=asc[an][:, g, P * a : P * (a + 1)],
-                        rhs=wc[name][:, g, cols].bitcast(FP8X4),
-                        rhs_scale=ws[name][:, g, cols],
-                        start=(first[(op, arg[3])] == i),
-                        stop=(last[(op, arg[3])] == i),
-                    )
-            elif op == "A":
-                j, a = int(arg[0]), int(arg[1])
-                z = outp.tile([P, HALF], F32, name="z", tag="z")
-                z_of[arg] = z
-                nc.vector.tensor_tensor(
-                    out=z[:], in0=banks[("acc2", j, a)][:], in1=bh_bc[:, HALF * j : HALF * (j + 1)], op=ALU.add
-                )
-            elif op == "T":
-                j, a = int(arg[0]), int(arg[1])
-                z = z_of[arg]
-                nc.scalar.activation(out=z[:], in_=z[:], func=ACT.Tanh)
-                nc.sync.dma_start(out=out_rows[:, a, HALF * j : HALF * (j + 1)], in_=z[:])
+
+        def gate(g):
+            nc.vector.tensor_tensor(
+                out=grouped["g"][g][:].rearrange("p (c i t) -> p c t i", i=4, t=PACK),
+                in0=r_runs[g][:],
+                in1=grouped["h"][g][:].rearrange("p (c i t) -> p c t i", i=4, t=PACK),
+                op=ALU.mult,
+            )
+
+        for i in range(len(UNITS) + 2):
+            if i < 2:
+                evacuate("h", i)
+            if i == 2:
+                quantise_activation("h", 0)
+                quantise_activation("h", 1)
+            if i < len(UNITS):
+                regroup(i)
+            if 1 <= i <= len(UNITS):
+                quantise(i - 1)
+            if i >= 2:
+                multiply(i - 2)
+            if i in (STAGE_2, STAGE_2 + 1):
+                sigmoid(i - STAGE_2)
+            if i in (STAGE_2 + 1, STAGE_2 + 2):
+                gate(i - STAGE_2 - 1)
+            if i == STAGE_2 + 2:
+                quantise_activation("g", 0)
+                quantise_activation("g", 1)
+
+        out_rows = out.rearrange("(p a) n -> p a n", a=TILES)
+        for j in range(2):
+            cols = slice(UNIT * j, UNIT * (j + 1))
+            for a in range(TILES):
+                result = results.tile([P, UNIT], F32, name="result", tag="result")
+                nc.vector.tensor_tensor(out=result[:], in0=sums[("out", j, a)][:], in1=bh_all[:, cols], op=ALU.add)
+                nc.scalar.activation(out=result[:], in_=result[:], func=ACT.Tanh)
+                nc.sync.dma_start(out=out_rows[:, a, cols], in_=result[:])

@@ -20,21 +20,22 @@ PASSES = 2
 BATCH = 512
 WIDTH = 1024
 UNIT = 512
+HALF = UNIT // 2
 TILES = UNIT // P
 
-UNITS = [(name, g, half) for name in ("W_r", "U_r", "W_h", "U_h") for g in range(PASSES) for half in range(2)]
-MOVING_WITH = {"W_r": "x", "U_r": "h", "W_h": "x", "U_h": "g"}
+UNITS = [(name, g, half) for name in ("W_r", "U_r", "W_h") for g in range(PASSES) for half in range(2)] + [
+    ("U_h", g, half) for half in range(2) for g in range(PASSES)
+]
+ACTIVATION_OF = {"W_r": "x", "U_r": "h", "W_h": "x", "U_h": "g"}
 STAGE_2 = 8
 
-VECTOR_SHARE = 224
 
-
-def vector_share(i):
-    if i in (STAGE_2, STAGE_2 + 1):
-        return UNIT
-    if i in (STAGE_2 + 2, STAGE_2 + 3):
-        return 0
-    return VECTOR_SHARE
+def regrouping_engines(i):
+    if i in (STAGE_2 + 1, STAGE_2 + 2):
+        return ("vector", "vector")
+    if i in (STAGE_2, STAGE_2 + 3, STAGE_2 + 4):
+        return ("scalar", "scalar")
+    return ("vector", "scalar")
 
 
 def tile_joint_gru_pa_kernel(tc, joint_h, mgn_h, W_r, W_h, U_r, U_h, b_r, b_h, out):
@@ -51,19 +52,13 @@ def tile_joint_gru_pa_kernel(tc, joint_h, mgn_h, W_r, W_h, U_r, U_h, b_r, b_h, o
         def bank(i, shape, dtype, name):
             return psum.tile(shape, dtype, name=name, tag="bank%d" % i)
 
-        br_rows = const.tile([P, P], BF16, name="br_rows")
+        br_rows = const.tile([P, 2 * P], BF16, name="br_rows")
         nc.vector.memset(br_rows[:].bitcast(I32), 0)
-        bh_row = const.tile([P, WIDTH], BF16, name="bh_row")
-        nc.vector.memset(bh_row[:].bitcast(I32), 0)
         warm = const.tile([P, 8], F32, name="warm")
         nc.vector.memset(warm[:], 0.0)
         nc.scalar.activation(out=warm[:, 4:5], in_=warm[:, 0:1], func=ACT.Sigmoid)
-        ident_f = const.tile([P, P], F32, name="ident_f")
-        make_identity(nc, ident_f[:])
-        ident_b = const.tile([P, P], BF16, name="ident_b")
-        make_identity(nc, ident_b[:])
-        ones_b = const.tile([P, P], BF16, name="ones_b")
-        nc.gpsimd.memset(ones_b[:], 1.0)
+        identity = const.tile([P, P], F32, name="identity")
+        make_identity(nc, identity[:])
 
         act_raw = {}
         for name, src in (("x", mgn_h), ("h", joint_h)):
@@ -71,20 +66,17 @@ def tile_joint_gru_pa_kernel(tc, joint_h, mgn_h, W_r, W_h, U_r, U_h, b_r, b_h, o
             rows = src.rearrange("(p a) k -> p a k", a=TILES)
             for pair in range(2):
                 nc.sync.dma_start(out=act_raw[name][:, 2 * pair : 2 * pair + 2, :], in_=rows[:, 2 * pair : 2 * pair + 2, :])
-        nc.sync.dma_start(out=br_rows[0 : WIDTH // P, :], in_=b_r.rearrange("(m p) -> m p", p=P))
-        nc.sync.dma_start(out=bh_row[0:1, :], in_=b_h.rearrange("(o n) -> o n", o=1))
+        nc.sync.dma_start(out=br_rows[0:4, :], in_=b_r.rearrange("(c n) -> c n", c=4))
         weight_raw = {}
         for name, src in (("W_r", W_r), ("U_r", U_r), ("W_h", W_h), ("U_h", U_h)):
             weight_raw[name] = raw.tile([P, PASSES, PACK, WIDTH], BF16, name="raw_" + name)
             for g in range(PASSES):
-                rows = src[UNIT * g : UNIT * (g + 1), :]
-                if name[0] == "W":
-                    nc.sync.dma_start(
-                        out=weight_raw[name][:, g].rearrange("q (u e) n -> q u (e n)", u=2),
-                        in_=rows.rearrange("(u q e) n -> q u (e n)", u=2, q=P, e=2),
-                    )
-                else:
-                    nc.sync.dma_start(out=weight_raw[name][:, g], in_=rows.rearrange("(t p) n -> p t n", p=P))
+                nc.sync.dma_start(
+                    out=weight_raw[name][:, g].rearrange("q (u e) n -> q u (e n)", u=2),
+                    in_=src[UNIT * g : UNIT * (g + 1), :].rearrange("(u q e) n -> q u (e n)", u=2, q=P, e=2),
+                )
+        bh_all = const.tile([P, WIDTH], BF16, name="bh_all")
+        nc.sync.dma_start(out=bh_all[:], in_=b_h.partition_broadcast(P))
 
         words = {}
         scales = {}
@@ -95,14 +87,13 @@ def tile_joint_gru_pa_kernel(tc, joint_h, mgn_h, W_r, W_h, U_r, U_h, b_r, b_h, o
         for name in ("x", "h", "g"):
             words[name] = keep.tile([P, PASSES, BATCH], U32, name="words_" + name, align_bytes=64)
             scales[name] = keep.tile([P, PASSES, BATCH], U8, name="scales_" + name, align_bytes=64)
-            grouped[name] = [
-                keep.tile([P, PACK * BATCH], BF16, name="grouped_%s%d" % (name, g), align_bytes=64)
-                for g in range(PASSES)
-            ]
+            grouped[name] = keep.tile([P, PASSES, PACK * BATCH], BF16, name="grouped_" + name, align_bytes=64)
 
-        def quantise_activation(name, g):
+        def quantise_activation(name):
             nc.vector.quantize_mx(
-                out=words[name][:, g, :].bitcast(FP8X4), scales=scales[name][:, g, :], in_=grouped[name][g][:]
+                out=words[name][:].rearrange("q g b -> q (g b)").bitcast(FP8X4),
+                scales=scales[name][:].rearrange("q g b -> q (g b)"),
+                in_=grouped[name][:].rearrange("q g n -> q (g n)"),
             )
 
         def copy(engine, dst, src):
@@ -112,79 +103,48 @@ def tile_joint_gru_pa_kernel(tc, joint_h, mgn_h, W_r, W_h, U_r, U_h, b_r, b_h, o
                 nc.scalar.copy(out=dst, in_=src)
 
         transposed = {}
-        for pair in range(2):
-            for g in range(PASSES):
-                xt = bank(2 * pair + g, [P, 2, 2, P], F32, "xt")
-                transposed[("x", pair, g)] = xt
-                for c in range(2):
-                    pairs_of_k = act_raw["x"][:, 2 * pair + c, :].bitcast(F32)
-                    for u in range(2):
-                        first = P * (2 * g + u)
-                        nc.tensor.transpose(xt[:, c, u, :], pairs_of_k[:, first : first + P], ident_f[:])
-        for pair in range(2):
-            for g in range(PASSES):
-                ht = bank(4 + 2 * pair + g, [P, 2, PACK, P], BF16, "ht")
-                transposed[("h", pair, g)] = ht
-                for c in range(2):
-                    for t in range(PACK):
-                        first = UNIT * g + P * t
-                        nc.tensor.transpose(ht[:, c, t, :], act_raw["h"][:, 2 * pair + c, first : first + P], ident_b[:])
+        for first_bank, name in ((0, "x"), (4, "h")):
+            for pair in range(2):
+                for g in range(PASSES):
+                    block = bank(first_bank + 2 * pair + g, [P, 2, 2, P], F32, "transposed")
+                    transposed[(name, pair, g)] = block
+                    for c in range(2):
+                        pairs_of_k = act_raw[name][:, 2 * pair + c, :].bitcast(F32)
+                        for u in range(2):
+                            first = P * (2 * g + u)
+                            nc.tensor.transpose(block[:, c, u, :], pairs_of_k[:, first : first + P], identity[:])
 
-        def evacuate(name, pair):
-            for g, engine in enumerate(("vector", "scalar")):
-                if name == "x":
-                    copy(
-                        engine,
-                        grouped["x"][g][:]
+        for name in ("x", "h"):
+            for pair in range(2):
+                for g in range(PASSES):
+                    nc.scalar.copy(
+                        out=grouped[name][:, g, :]
                         .bitcast(F32)[:, UNIT * pair : UNIT * (pair + 1)]
                         .rearrange("q (c b u) -> q c b u", c=2, b=P, u=2),
-                        transposed[("x", pair, g)][:].rearrange("q c u b -> q c b u"),
+                        in_=transposed[(name, pair, g)][:].rearrange("q c u b -> q c b u"),
                     )
-                else:
-                    copy(
-                        engine,
-                        grouped["h"][g][:, 2 * UNIT * pair : 2 * UNIT * (pair + 1)].rearrange(
-                            "p (c b t) -> p c b t", c=2, b=P, t=PACK
-                        ),
-                        transposed[("h", pair, g)][:].rearrange("p c t b -> p c b t"),
-                    )
+        quantise_activation("x")
 
-        evacuate("x", 0)
-        evacuate("x", 1)
-        quantise_activation("x", 0)
-        quantise_activation("x", 1)
-
-        br_ps = bank(0, [P, P], BF16, "br_ps")
-        nc.tensor.transpose(br_ps[:], br_rows[:], ident_b[:])
+        br_ps = bank(0, [P, P], F32, "br_ps")
+        nc.tensor.transpose(br_ps[:], br_rows[:].bitcast(F32), identity[:])
         br_col = const.tile([P, WIDTH // P], F32, name="br_col")
-        nc.vector.tensor_copy(out=br_col[:], in_=br_ps[:, 0 : WIDTH // P])
-        bh_ps = bank(1, [P, WIDTH], BF16, "bh_ps")
-        for j in range(2):
-            nc.tensor.matmul(
-                out=bh_ps[:, UNIT * j : UNIT * (j + 1)],
-                lhsT=ones_b[:],
-                rhs=bh_row[:, UNIT * j : UNIT * (j + 1)],
-                start=True,
-                stop=True,
-            )
-        bh_all = const.tile([P, WIDTH], BF16, name="bh_all")
-        nc.scalar.copy(out=bh_all[:], in_=bh_ps[:])
+        nc.vector.tensor_copy(out=br_col[:], in_=br_ps[:, 0:4].bitcast(BF16))
 
         unit_tile = {}
 
         def regroup(i):
             name, g, half = UNITS[i]
             unit_tile[i] = regrouped.tile([P, UNIT, PACK], BF16, name="unit", tag="unit", align_bytes=64)
-            split = vector_share(i)
-            for engine, lo, hi in (("scalar", split, UNIT), ("vector", 0, split)):
-                if lo < hi:
-                    copy(
-                        engine,
-                        unit_tile[i][:, lo:hi, :].rearrange("p (c i) t -> p c t i", i=4),
-                        weight_raw[name][:, g, :, UNIT * half + lo : UNIT * half + hi].rearrange(
-                            "p t (c i) -> p c t i", i=4
-                        ),
-                    )
+            for part in (1, 0):
+                dst = unit_tile[i][:, HALF * part : HALF * (part + 1), :]
+                src = weight_raw[name][:, g, :, UNIT * half + HALF * part : UNIT * half + HALF * (part + 1)]
+                if i < STAGE_2:
+                    dst = dst.rearrange("q (e n) t -> q n t e", e=2)
+                    src = src.rearrange("q t (n e) -> q n t e", e=2)
+                else:
+                    dst = dst.rearrange("q (c i) t -> q c t i", i=4)
+                    src = src.rearrange("q t (c i) -> q c t i", i=4)
+                copy(regrouping_engines(i)[part], dst, src)
 
         def quantise(i):
             name, g, half = UNITS[i]
@@ -192,14 +152,14 @@ def tile_joint_gru_pa_kernel(tc, joint_h, mgn_h, W_r, W_h, U_r, U_h, b_r, b_h, o
             nc.vector.quantize_mx(
                 out=words[name][:, g, cols].bitcast(FP8X4),
                 scales=scales[name][:, g, cols],
-                in_=unit_tile[i][:].rearrange("p n t -> p (n t)"),
+                in_=unit_tile[i][:].rearrange("q n t -> q (n t)"),
             )
 
         sums = {}
 
         def multiply(i):
             name, g, half = UNITS[i]
-            act = MOVING_WITH[name]
+            act = ACTIVATION_OF[name]
             opens = name[0] == "W" and g == 0
             closes = name[0] == "U" and g == PASSES - 1
             for tile in range(TILES):
@@ -225,12 +185,12 @@ def tile_joint_gru_pa_kernel(tc, joint_h, mgn_h, W_r, W_h, U_r, U_h, b_r, b_h, o
 
         r_runs = [keep.tile([P, BATCH // 4, PACK, 4], F32, name="r_runs%d" % g) for g in range(PASSES)]
 
-        def sigmoid(half):
-            for t in range(TILES):
-                m = TILES * half + t
+        def sigmoid(g):
+            for t in range(PACK):
+                m = PACK * g + t
                 nc.scalar.activation(
-                    out=r_runs[half][:, :, t, :],
-                    in_=sums[("r", m)][:].rearrange("p (c i) -> p c i", i=4),
+                    out=r_runs[g][:, :, t, :],
+                    in_=sums[("r", m)][:].rearrange("q (c i) -> q c i", i=4),
                     func=ACT.Sigmoid,
                     bias=br_col[:, m : m + 1],
                     scale=1.0,
@@ -238,31 +198,27 @@ def tile_joint_gru_pa_kernel(tc, joint_h, mgn_h, W_r, W_h, U_r, U_h, b_r, b_h, o
 
         def gate(g):
             nc.vector.tensor_tensor(
-                out=grouped["g"][g][:].rearrange("p (c i t) -> p c t i", i=4, t=PACK),
+                out=grouped["g"][:, g, :].rearrange("q (c i t) -> q c t i", i=4, t=PACK),
                 in0=r_runs[g][:],
-                in1=grouped["h"][g][:].rearrange("p (c i t) -> p c t i", i=4, t=PACK),
+                in1=grouped["h"][:, g, :].rearrange("q (c i t) -> q c t i", i=4, t=PACK),
                 op=ALU.mult,
             )
 
         for i in range(len(UNITS) + 2):
-            if i < 2:
-                evacuate("h", i)
-            if i == 2:
-                quantise_activation("h", 0)
-                quantise_activation("h", 1)
             if i < len(UNITS):
                 regroup(i)
+            if i == 1:
+                quantise_activation("h")
             if 1 <= i <= len(UNITS):
                 quantise(i - 1)
             if i >= 2:
                 multiply(i - 2)
             if i in (STAGE_2, STAGE_2 + 1):
                 sigmoid(i - STAGE_2)
-            if i in (STAGE_2 + 1, STAGE_2 + 2):
-                gate(i - STAGE_2 - 1)
-            if i == STAGE_2 + 2:
-                quantise_activation("g", 0)
-                quantise_activation("g", 1)
+            if i in (STAGE_2 + 2, STAGE_2 + 3):
+                gate(i - STAGE_2 - 2)
+            if i == STAGE_2 + 3:
+                quantise_activation("g")
 
         out_rows = out.rearrange("(p a) n -> p a n", a=TILES)
         for j in range(2):

from contextlib import ExitStack

import concourse.mybir as mybir
from concourse.masks import make_identity

FLOPS = 4 * 2 * 512 * 1024 * 1024

F32 = mybir.dt.float32
BF16 = mybir.dt.bfloat16
I32 = mybir.dt.int32
U32 = mybir.dt.uint32
U8 = mybir.dt.uint8
FP8X4 = mybir.dt.float8_e4m3fn_x4
ACT = mybir.ActivationFunctionType
ALU = mybir.AluOpType

P = 128
PACK = 4
PASSES = 2
BATCH = 512
WIDTH = 1024
UNIT = 512
HALF = UNIT // 2
TILES = UNIT // P

UNITS = [(name, g, half) for name in ("W_r", "U_r", "W_h") for g in range(PASSES) for half in range(2)] + [
    ("U_h", g, half) for half in range(2) for g in range(PASSES)
]
ACTIVATION_OF = {"W_r": "x", "U_r": "h", "W_h": "x", "U_h": "g"}
STAGE_2 = 8


def regrouping_engines(i):
    if i in (STAGE_2 + 1, STAGE_2 + 2):
        return ("vector", "vector")
    if i in (STAGE_2, STAGE_2 + 3, STAGE_2 + 4):
        return ("scalar", "scalar")
    return ("vector", "scalar")


def tile_joint_gru_pa_kernel(tc, joint_h, mgn_h, W_r, W_h, U_r, U_h, b_r, b_h, out):
    nc = tc.nc
    with ExitStack() as ctx:
        const = ctx.enter_context(tc.tile_pool(name="const", bufs=1))
        raw = ctx.enter_context(tc.tile_pool(name="raw", bufs=1))
        keep = ctx.enter_context(tc.tile_pool(name="keep", bufs=1))
        regrouped = ctx.enter_context(tc.tile_pool(name="regrouped", bufs=6))
        results = ctx.enter_context(tc.tile_pool(name="results", bufs=8))
        psum = ctx.enter_context(tc.psum_pool(name="psum", bufs=1))
        ctx.enter_context(tc.manual_schedule())

        def bank(i, shape, dtype, name):
            return psum.tile(shape, dtype, name=name, tag="bank%d" % i)

        br_rows = const.tile([P, 2 * P], BF16, name="br_rows")
        nc.vector.memset(br_rows[:].bitcast(I32), 0)
        warm = const.tile([P, 8], F32, name="warm")
        nc.vector.memset(warm[:], 0.0)
        nc.scalar.activation(out=warm[:, 4:5], in_=warm[:, 0:1], func=ACT.Sigmoid)
        identity = const.tile([P, P], F32, name="identity")
        make_identity(nc, identity[:])

        act_raw = {}
        for name, src in (("x", mgn_h), ("h", joint_h)):
            act_raw[name] = raw.tile([P, TILES, WIDTH], BF16, name="raw_" + name)
            rows = src.rearrange("(p a) k -> p a k", a=TILES)
            for pair in range(2):
                nc.sync.dma_start(out=act_raw[name][:, 2 * pair : 2 * pair + 2, :], in_=rows[:, 2 * pair : 2 * pair + 2, :])
        nc.sync.dma_start(out=br_rows[0:4, :], in_=b_r.rearrange("(c n) -> c n", c=4))
        weight_raw = {}
        for name, src in (("W_r", W_r), ("U_r", U_r), ("W_h", W_h), ("U_h", U_h)):
            weight_raw[name] = raw.tile([P, PASSES, PACK, WIDTH], BF16, name="raw_" + name)
            for g in range(PASSES):
                nc.sync.dma_start(
                    out=weight_raw[name][:, g].rearrange("q (u e) n -> q u (e n)", u=2),
                    in_=src[UNIT * g : UNIT * (g + 1), :].rearrange("(u q e) n -> q u (e n)", u=2, q=P, e=2),
                )
        bh_all = const.tile([P, WIDTH], BF16, name="bh_all")
        nc.sync.dma_start(out=bh_all[:], in_=b_h.partition_broadcast(P))

        words = {}
        scales = {}
        for name in ("W_r", "U_r", "W_h", "U_h"):
            words[name] = keep.tile([P, PASSES, WIDTH], U32, name="words_" + name, align_bytes=64)
            scales[name] = keep.tile([P, PASSES, WIDTH], U8, name="scales_" + name, align_bytes=64)
        grouped = {}
        for name in ("x", "h", "g"):
            words[name] = keep.tile([P, PASSES, BATCH], U32, name="words_" + name, align_bytes=64)
            scales[name] = keep.tile([P, PASSES, BATCH], U8, name="scales_" + name, align_bytes=64)
            grouped[name] = keep.tile([P, PASSES, PACK * BATCH], BF16, name="grouped_" + name, align_bytes=64)

        def quantise_activation(name):
            nc.vector.quantize_mx(
                out=words[name][:].rearrange("q g b -> q (g b)").bitcast(FP8X4),
                scales=scales[name][:].rearrange("q g b -> q (g b)"),
                in_=grouped[name][:].rearrange("q g n -> q (g n)"),
            )

        def copy(engine, dst, src):
            if engine == "vector":
                nc.vector.tensor_copy(out=dst, in_=src)
            else:
                nc.scalar.copy(out=dst, in_=src)

        transposed = {}
        for first_bank, name in ((0, "x"), (4, "h")):
            for pair in range(2):
                for g in range(PASSES):
                    block = bank(first_bank + 2 * pair + g, [P, 2, 2, P], F32, "transposed")
                    transposed[(name, pair, g)] = block
                    for c in range(2):
                        pairs_of_k = act_raw[name][:, 2 * pair + c, :].bitcast(F32)
                        for u in range(2):
                            first = P * (2 * g + u)
                            nc.tensor.transpose(block[:, c, u, :], pairs_of_k[:, first : first + P], identity[:])

        for name in ("x", "h"):
            for pair in range(2):
                for g in range(PASSES):
                    nc.scalar.copy(
                        out=grouped[name][:, g, :]
                        .bitcast(F32)[:, UNIT * pair : UNIT * (pair + 1)]
                        .rearrange("q (c b u) -> q c b u", c=2, b=P, u=2),
                        in_=transposed[(name, pair, g)][:].rearrange("q c u b -> q c b u"),
                    )
        quantise_activation("x")

        br_ps = bank(0, [P, P], F32, "br_ps")
        nc.tensor.transpose(br_ps[:], br_rows[:].bitcast(F32), identity[:])
        br_col = const.tile([P, WIDTH // P], F32, name="br_col")
        nc.vector.tensor_copy(out=br_col[:], in_=br_ps[:, 0:4].bitcast(BF16))

        unit_tile = {}

        def regroup(i):
            name, g, half = UNITS[i]
            unit_tile[i] = regrouped.tile([P, UNIT, PACK], BF16, name="unit", tag="unit", align_bytes=64)
            for part in (1, 0):
                dst = unit_tile[i][:, HALF * part : HALF * (part + 1), :]
                src = weight_raw[name][:, g, :, UNIT * half + HALF * part : UNIT * half + HALF * (part + 1)]
                if i < STAGE_2:
                    dst = dst.rearrange("q (e n) t -> q n t e", e=2)
                    src = src.rearrange("q t (n e) -> q n t e", e=2)
                else:
                    dst = dst.rearrange("q (c i) t -> q c t i", i=4)
                    src = src.rearrange("q t (c i) -> q c t i", i=4)
                copy(regrouping_engines(i)[part], dst, src)

        def quantise(i):
            name, g, half = UNITS[i]
            cols = slice(UNIT * half, UNIT * (half + 1))
            nc.vector.quantize_mx(
                out=words[name][:, g, cols].bitcast(FP8X4),
                scales=scales[name][:, g, cols],
                in_=unit_tile[i][:].rearrange("q n t -> q (n t)"),
            )

        sums = {}

        def multiply(i):
            name, g, half = UNITS[i]
            act = ACTIVATION_OF[name]
            opens = name[0] == "W" and g == 0
            closes = name[0] == "U" and g == PASSES - 1
            for tile in range(TILES):
                if i < STAGE_2:
                    key = ("r", TILES * half + tile)
                    stationary, s_cols = name, slice(UNIT * half + P * tile, UNIT * half + P * (tile + 1))
                    moving, m_cols = act, slice(0, BATCH)
                else:
                    key = ("out", half, tile)
                    stationary, s_cols = act, slice(P * tile, P * (tile + 1))
                    moving, m_cols = name, slice(UNIT * half, UNIT * (half + 1))
                if opens:
                    sums[key] = bank(TILES * half + tile, [P, UNIT], F32, "sums")
                nc.tensor.matmul_mx(
                    out=sums[key][:],
                    lhsT=words[stationary][:, g, s_cols].bitcast(FP8X4),
                    lhsT_scale=scales[stationary][:, g, s_cols],
                    rhs=words[moving][:, g, m_cols].bitcast(FP8X4),
                    rhs_scale=scales[moving][:, g, m_cols],
                    start=opens,
                    stop=closes,
                )

        r_runs = [keep.tile([P, BATCH // 4, PACK, 4], F32, name="r_runs%d" % g) for g in range(PASSES)]

        def sigmoid(g):
            for t in range(PACK):
                m = PACK * g + t
                nc.scalar.activation(
                    out=r_runs[g][:, :, t, :],
                    in_=sums[("r", m)][:].rearrange("q (c i) -> q c i", i=4),
                    func=ACT.Sigmoid,
                    bias=br_col[:, m : m + 1],
                    scale=1.0,
                )

        def gate(g):
            nc.vector.tensor_tensor(
                out=grouped["g"][:, g, :].rearrange("q (c i t) -> q c t i", i=4, t=PACK),
                in0=r_runs[g][:],
                in1=grouped["h"][:, g, :].rearrange("q (c i t) -> q c t i", i=4, t=PACK),
                op=ALU.mult,
            )

        for i in range(len(UNITS) + 2):
            if i < len(UNITS):
                regroup(i)
            if i == 1:
                quantise_activation("h")
            if 1 <= i <= len(UNITS):
                quantise(i - 1)
            if i >= 2:
                multiply(i - 2)
            if i in (STAGE_2, STAGE_2 + 1):
                sigmoid(i - STAGE_2)
            if i in (STAGE_2 + 2, STAGE_2 + 3):
                gate(i - STAGE_2 - 2)
            if i == STAGE_2 + 3:
                quantise_activation("g")

        out_rows = out.rearrange("(p a) n -> p a n", a=TILES)
        for j in range(2):
            cols = slice(UNIT * j, UNIT * (j + 1))
            for a in range(TILES):
                result = results.tile([P, UNIT], F32, name="result", tag="result")
                nc.vector.tensor_tensor(out=result[:], in0=sums[("out", j, a)][:], in1=bh_all[:, cols], op=ALU.add)
                nc.scalar.activation(out=result[:], in_=result[:], func=ACT.Tanh)
                nc.sync.dma_start(out=out_rows[:, a, cols], in_=result[:])
